import numpy as np
import ml_dtypes


def mxq(x, axis, fmt="e4m3"):
    dtype, down = {"e4m3": (ml_dtypes.float8_e4m3fn, 7), "e5m2": (ml_dtypes.float8_e5m2, 14)}[fmt]
    v = np.moveaxis(np.asarray(x, np.float32).astype(ml_dtypes.bfloat16).astype(np.float64), axis, -1)
    blocks = v.reshape(v.shape[:-1] + (-1, 32))
    amax = np.abs(blocks).max(-1, keepdims=True)
    byte = np.maximum(np.where(amax > 0, np.frexp(amax)[1] - 1 + 127, 0) - down, 1)
    scale = np.exp2(byte - 127.0)
    codes = (blocks / scale).astype(np.float32).astype(dtype).astype(np.float64)
    return np.moveaxis((codes * scale).reshape(v.shape), -1, axis)


WIDE = False


def mx_kscale(k):
    if not WIDE:
        return np.ones(k)
    levels = np.array([18, -18])
    if k % 512:
        return np.exp2(np.random.permutation(np.resize(levels, k // 32))).repeat(32)
    a = np.empty((k // 512, 16))
    for p in range(k // 512):
        a[p, :8] = np.random.permutation(np.resize(levels, 8))
        for g in range(8):
            far = levels[np.abs(levels - a[p, g]) >= 10]
            a[p, g + 8] = far[np.random.randint(len(far))]
    return np.exp2(a.ravel()).repeat(32)


BF16 = ml_dtypes.bfloat16


def bf(x):
    return np.asarray(x, np.float32).astype(BF16)


def f64(x):
    return np.asarray(x).astype(np.float64)


B, K, F, INCH, OUTCH, R = 2, 4, 128, 1024, 2048, 128
T = B * K * F


def erf(a):
    c = np.clip(a, -6.0, 6.0)
    c2 = 2.0 * c * c
    t = c.copy()
    s = c.copy()
    n = 1.0
    while np.max(np.abs(t) - 1e-18 * np.abs(s)) > 0.0:
        n += 2.0
        t = t * c2 / n
        s = s + t
    return 2.0 / np.sqrt(np.pi) * np.exp(-c * c) * s


def gelu(t):
    return 0.5 * t * (1.0 + erf(t / np.sqrt(2.0)))


def gelu_grad(t):
    return 0.5 * (1.0 + erf(t / np.sqrt(2.0))) + t * np.exp(-0.5 * t * t) / np.sqrt(2.0 * np.pi)


def setup_inputs():
    s = mx_kscale(T).reshape(B, K, F, 1)
    o = mx_kscale(OUTCH)
    h0 = bf(gelu(np.random.standard_normal((B, K, F, INCH))))
    z = bf(np.random.standard_normal((B, K, F, R)) * 0.35)
    u = bf(np.random.standard_normal((B, K, OUTCH, R)) * 1.5 * np.sqrt(R))
    b = bf(np.random.standard_normal((B, 1, 1, OUTCH)) * 0.3)
    w0 = bf(np.random.standard_normal((OUTCH, INCH)) * 1.5 / np.sqrt(INCH))
    b_out = bf(np.random.standard_normal(OUTCH) * 0.3)
    g = bf(np.random.standard_normal((B, K, F, OUTCH)) * 2.0 * np.exp2(np.random.randint(-6, 1, (B, K, F, 1))) / s * o)
    lora = f64(z) @ f64(u).transpose(0, 1, 3, 2) / R
    pre = f64(h0) @ f64(w0).T + f64(b_out) + lora + f64(b)
    return {
        "h": bf(f64(h0) * s),
        "z": z,
        "u": u,
        "b": b,
        "W_out": bf(f64(w0) / o[:, None]),
        "b_out": b_out,
        "pre": np.asarray(pre, np.float32),
        "grad_out": g,
    }


def reference(h, z, u, b, W_out, b_out, pre, grad_out):
    dz = (f64(grad_out) * gelu_grad(f64(pre))).reshape(T, OUTCH)
    ht = f64(h).reshape(T, INCH)
    dh = mxq(dz, 1, "e5m2") @ mxq(f64(W_out), 0, "e4m3")
    dw = mxq(dz, 0, "e5m2").T @ mxq(ht, 0, "e4m3")
    return dh.reshape(B, K, F, INCH), dw

@@ -1,0 +1,298 @@
+from contextlib import ExitStack
+
+import concourse.mybir as mybir
+from concourse.masks import make_identity
+
+TOKENS, OUTCH, INCH = 1024, 2048, 1024
+FLOPS = 2 * 2 * TOKENS * OUTCH * INCH
+BYTES = 2 * (TOKENS * INCH + OUTCH * INCH + TOKENS * OUTCH) + 4 * (
+    TOKENS * OUTCH + TOKENS * INCH + OUTCH * INCH
+)
+
+F32 = mybir.dt.float32
+BF16 = mybir.dt.bfloat16
+U32 = mybir.dt.uint32
+U8 = mybir.dt.uint8
+E4M3 = mybir.dt.float8_e4m3fn_x4
+E5M2 = mybir.dt.float8_e5m2_x4
+ALU = mybir.AluOpType
+ACT = mybir.ActivationFunctionType
+
+P = 128
+K_PASS = 512
+N_TILE = 512
+GROUPS = TOKENS // K_PASS
+CHUNKS = OUTCH // K_PASS
+HALVES = INCH // N_TILE
+UNITS = GROUPS * CHUNKS
+STEPS = 2 * UNITS
+
+H = 2.0**-7
+CLAMP = 9.0
+OFFSETS = (H, -H, 2.0 * H, -2.0 * H)
+
+
+def tile_loratacmlp4_pb_v_kernel(
+    tc, h, z, u, b, W_out, b_out, pre, grad_out, out_0, out_1
+):
+    nc = tc.nc
+    h_rows = h.flatten_outer_dims()
+    pre_rows = pre.flatten_outer_dims()
+    grad_rows = grad_out.flatten_outer_dims()
+    dh_rows = out_0.flatten_outer_dims()
+
+    with ExitStack() as ctx:
+        keep = ctx.enter_context(tc.tile_pool(name="keep", bufs=1))
+        work = ctx.enter_context(tc.tile_pool(name="work", bufs=2))
+        psum = ctx.enter_context(tc.psum_pool(name="psum", bufs=2))
+
+        offs = keep.tile([P, 4], F32, name="offs")
+        for k in range(4):
+            nc.vector.memset(offs[:, k : k + 1], OFFSETS[k])
+        warm = keep.tile([P, 1], F32, name="warm")
+        nc.scalar.activation(out=warm[:], in_=offs[:, 0:1], func=ACT.Gelu, bias=offs[:, 0:1], scale=1.0)
+        ident = keep.tile([P, P], F32, name="ident")
+        make_identity(nc, ident[:])
+
+        w_codes = keep.tile([P, CHUNKS, INCH], U32, name="w_codes", align_bytes=64)
+        w_scales = keep.tile([P, CHUNKS, INCH], U8, name="w_scales", align_bytes=64)
+        h_codes = keep.tile([P, GROUPS, INCH], U32, name="h_codes", align_bytes=64)
+        h_scales = keep.tile([P, GROUPS, INCH], U8, name="h_scales", align_bytes=64)
+        tok_codes = keep.tile([P, UNITS, K_PASS], U32, name="tok_codes", align_bytes=64)
+        tok_scales = keep.tile([P, UNITS, K_PASS], U8, name="tok_scales", align_bytes=64)
+        fea_codes = keep.tile([P, UNITS, K_PASS], U32, name="fea_codes", align_bytes=64)
+        fea_scales = keep.tile([P, UNITS, K_PASS], U8, name="fea_scales", align_bytes=64)
+
+        pre_t, grad_t, t_bank, gel, y_t, m_bank, dz_t = {}, {}, {}, {}, {}, {}, {}
+
+        def where(s):
+            unit = s // 2
+            return unit // CHUNKS, unit % CHUNKS, s % 2
+
+        def load_step(s):
+            if s >= STEPS:
+                return
+            g, c, half = where(s)
+            rows = slice(g * K_PASS, (g + 1) * K_PASS)
+            cols = slice(c * K_PASS, (c + 1) * K_PASS)
+            pre_t[s] = work.tile([P, 2, K_PASS], F32, name="pre_t", bufs=4)
+            nc.sync.dma_start(
+                out=pre_t[s][:],
+                in_=pre_rows[rows, cols].rearrange("(p j) w -> p j w", j=4)[:, 2 * half : 2 * half + 2, :],
+            )
+            if half == 0:
+                grad_t[s // 2] = work.tile([P, 4, K_PASS], BF16, name="grad_t", bufs=3)
+                nc.sync.dma_start(
+                    out=grad_t[s // 2][:],
+                    in_=grad_rows[rows, cols].rearrange("(p j) w -> p j w", j=4),
+                )
+
+        def clamp_step(s):
+            if s < STEPS:
+                nc.gpsimd.tensor_scalar(
+                    out=pre_t[s][:], in0=pre_t[s][:], scalar1=CLAMP, scalar2=-CLAMP, op0=ALU.min, op1=ALU.max
+                )
+
+        def transpose_in(s, bk):
+            bank = psum.tile([P, 4, P], F32, name="t_bank", bufs=2)
+            t_bank[s, bk] = bank
+            for fb in range(4):
+                nc.tensor.transpose(bank[:, fb, :], pre_t[s][:, bk, fb * P : (fb + 1) * P], ident[:])
+
+        def gelus(s, bk):
+            if bk == 0:
+                gel[s] = [work.tile([P, 2, K_PASS], F32, name="gel%d" % k, bufs=2) for k in range(4)]
+            for k in range(4):
+                nc.scalar.activation(
+                    out=gel[s][k][:, bk, :],
+                    in_=t_bank[s, bk][:].rearrange("p f q -> p (f q)"),
+                    func=ACT.Gelu,
+                    bias=offs[:, k : k + 1],
+                    scale=1.0,
+                )
+
+        def stencil(s):
+            gp1, gm1, gp2, gm2 = gel[s]
+            y1 = work.tile([P, 2, K_PASS], F32, name="y1", bufs=2)
+            y2 = work.tile([P, 2, K_PASS], F32, name="y2", bufs=2)
+            nc.vector.scalar_tensor_tensor(
+                out=y1[:], in0=gp1[:], scalar=8.0, in1=gp2[:], op0=ALU.mult, op1=ALU.subtract
+            )
+            nc.vector.scalar_tensor_tensor(
+                out=y2[:], in0=gm1[:], scalar=-8.0, in1=gm2[:], op0=ALU.mult, op1=ALU.add
+            )
+            y_t[s] = (y1, y2)
+
+        def combine(s, bk):
+            bank = psum.tile([P, K_PASS], F32, name="m_bank", bufs=2)
+            m_bank[s, bk] = bank
+            y1, y2 = y_t[s]
+            for fb in range(4):
+                cols = slice(fb * P, (fb + 1) * P)
+                nc.tensor.matmul(bank[:, cols], lhsT=y1[:, bk, cols], rhs=ident[:], start=True, stop=False, is_transpose=True)
+                nc.tensor.matmul(bank[:, cols], lhsT=y2[:, bk, cols], rhs=ident[:], start=False, stop=True, is_transpose=True)
+
+        def finish(s, bk):
+            unit, j = s // 2, 2 * (s % 2) + bk
+            if j == 0:
+                dz_t[unit] = work.tile([P, 4 * K_PASS], BF16, name="dz_t", bufs=2, align_bytes=64)
+            nc.vector.scalar_tensor_tensor(
+                out=dz_t[unit][:, j * K_PASS : (j + 1) * K_PASS],
+                in0=m_bank[s, bk][:],
+                scalar=1.0 / (12.0 * H),
+                in1=grad_t[unit][:, j, :],
+                op0=ALU.mult,
+                op1=ALU.mult,
+            )
+
+        pending_quant = []
+
+        def interleave_tokens(unit):
+            dst = work.tile([P, 4 * K_PASS], BF16, name="dz_tok", bufs=2, align_bytes=64)
+            nc.vector.tensor_copy(
+                out=dst[:].rearrange("p (c i t) -> p c t i", i=4, t=4),
+                in_=dz_t[unit][:].rearrange("p (t c i) -> p c t i", i=4, t=4),
+            )
+            pending_quant.append(
+                lambda: nc.vector.quantize_mx(
+                    out=tok_codes[:, unit, :].bitcast(E5M2), scales=tok_scales[:, unit, :], in_=dst[:]
+                )
+            )
+
+        def transpose_words(unit):
+            words = dz_t[unit][:].bitcast(F32)
+            dst = work.tile([P, 4 * K_PASS], BF16, name="dz_fea", bufs=2, align_bytes=64)
+            dst_words = dst[:].bitcast(F32).rearrange("p (j r u) -> p j r u", j=4, u=2)
+            for jp in range(2):
+                bank = psum.tile([P, 2, 2, P], F32, name="w_bank", bufs=1)
+                for j in range(2):
+                    base = (2 * jp + j) * (K_PASS // 2)
+                    for e in range(2):
+                        nc.tensor.transpose(bank[:, j, e, :], words[:, base + e : base + K_PASS // 2 : 2], ident[:])
+                nc.scalar.copy(
+                    out=dst_words[:, 2 * jp : 2 * jp + 2, :, :], in_=bank[:].rearrange("p j u r -> p j r u")
+                )
+            pending_quant.append(
+                lambda: nc.vector.quantize_mx(
+                    out=fea_codes[:, unit, :].bitcast(E5M2), scales=fea_scales[:, unit, :], in_=dst[:]
+                )
+            )
+
+        raw_t = {}
+
+        def load_raw(kind, i):
+            src = W_out if kind == "w" else h_rows
+            raw = work.tile([P, 4, INCH], BF16, name="raw", bufs=2)
+            nc.sync.dma_start(
+                out=raw[:], in_=src[i * K_PASS : (i + 1) * K_PASS, :].rearrange("(p j) n -> p j n", j=4)
+            )
+            raw_t[kind, i] = raw
+
+        def interleave_raw(kind, i, engine):
+            raw = raw_t[kind, i]
+            dst = work.tile([P, 4 * INCH], BF16, name="raw_i", bufs=2, align_bytes=64)
+            move = nc.vector.tensor_copy if engine == "v" else nc.scalar.copy
+            move(
+                out=dst[:].rearrange("p (c i t) -> p c t i", i=4, t=4),
+                in_=raw[:].rearrange("p t (c i) -> p c t i", i=4),
+            )
+            codes, scales = (w_codes, w_scales) if kind == "w" else (h_codes, h_scales)
+            pending_quant.append(
+                lambda: nc.vector.quantize_mx(out=codes[:, i, :].bitcast(E4M3), scales=scales[:, i, :], in_=dst[:])
+            )
+
+        ready, evacs = [], []
+        stage = {}
+
+        def mx_group(kind, row, m, n):
+            acc = psum.tile([P, N_TILE], F32, name="acc", bufs=3)
+            m_cols = slice(m * P, (m + 1) * P)
+            n_cols = slice(n * N_TILE, (n + 1) * N_TILE)
+            passes = CHUNKS if kind == "dh" else GROUPS
+            for k in range(passes):
+                if kind == "dh":
+                    unit = row * CHUNKS + k
+                    lc, ls, rc, rs = fea_codes, fea_scales, w_codes, w_scales
+                else:
+                    unit = k * CHUNKS + row
+                    lc, ls, rc, rs = tok_codes, tok_scales, h_codes, h_scales
+                nc.tensor.matmul_mx(
+                    out=acc[:],
+                    lhsT=lc[:, unit, m_cols].bitcast(E5M2),
+                    lhsT_scale=ls[:, unit, m_cols],
+                    rhs=rc[:, k, n_cols].bitcast(E4M3),
+                    rhs_scale=rs[:, k, n_cols],
+                    start=(k == 0),
+                    stop=(k == passes - 1),
+                )
+            evacs.append((kind, row, m, n, acc))
+
+        def evacuate(kind, row, m, n, acc):
+            n_cols = slice(n * N_TILE, (n + 1) * N_TILE)
+            if n == 0:
+                stage[kind, row, m] = work.tile([P, INCH], F32, name="stage", bufs=4)
+            dst = stage[kind, row, m]
+            if n == 0:
+                nc.scalar.copy(out=dst[:, n_cols], in_=acc[:])
+            else:
+                nc.vector.tensor_copy(out=dst[:, n_cols], in_=acc[:])
+            if n == HALVES - 1:
+                if kind == "dh":
+                    hbm = dh_rows[row * K_PASS : (row + 1) * K_PASS, :].rearrange("(p j) n -> p j n", j=4)[:, m, :]
+                else:
+                    hbm = out_1[row * K_PASS + m * P : row * K_PASS + (m + 1) * P, :]
+                nc.sync.dma_start(out=hbm, in_=dst[:])
+
+        def drain_mx(count):
+            for e in list(evacs):
+                evacuate(*e)
+            evacs.clear()
+            for i in range(min(count, len(ready))):
+                mx_group(*ready[i])
+            for i in range(min(count, len(ready))):
+                ready.remove(ready[0])
+
+        fills = [("w", 0), ("w", 1), ("w", 2), ("w", 3), ("h", 0), ("h", 1)]
+        engines = ["v", "s", "v", "s", "v", "v"]
+
+        for s in range(3):
+            load_step(s)
+        load_raw(*fills[0])
+        clamp_step(0)
+        step = 0
+        while step < STEPS + 4 or ready or evacs:
+            load_step(step + 3)
+            if step % 2 == 0 and step // 2 + 1 < len(fills):
+                load_raw(*fills[step // 2 + 1])
+            if step < STEPS:
+                clamp_step(step + 1)
+            new_ready = []
+            quants = list(pending_quant)
+            pending_quant.clear()
+            for bk in range(2):
+                if step < STEPS:
+                    transpose_in(step, bk)
+                    gelus(step, bk)
+                if 0 <= step - 2 < STEPS:
+                    combine(step - 2, bk)
+                    finish(step - 2, bk)
+                drain_mx(3)
+            if 0 <= step - 1 < STEPS:
+                stencil(step - 1)
+            for q in quants:
+                q()
+            if 0 <= step - 3 < STEPS and (step - 3) % 2 == 1:
+                unit = (step - 3) // 2
+                g, c = unit // CHUNKS, unit % CHUNKS
+                if c == CHUNKS - 1:
+                    new_ready += [("dh", g, m, n) for m in range(4) for n in range(HALVES)]
+                if g == GROUPS - 1:
+                    new_ready += [("dw", c, m, n) for m in range(4) for n in range(HALVES)]
+            ready += new_ready
+            if 0 <= step - 2 < STEPS and (step - 2) % 2 == 1:
+                unit = (step - 2) // 2
+                interleave_tokens(unit)
+                transpose_words(unit)
+            if step % 2 == 1 and step // 2 < len(fills):
+                interleave_raw(*fills[step // 2], engines[step // 2])
+            step += 1

@@ -5,9 +5,7 @@ from concourse.masks import make_identity
 
 TOKENS, OUTCH, INCH = 1024, 2048, 1024
 FLOPS = 2 * 2 * TOKENS * OUTCH * INCH
-BYTES = 2 * (TOKENS * INCH + OUTCH * INCH + TOKENS * OUTCH) + 4 * (
-    TOKENS * OUTCH + TOKENS * INCH + OUTCH * INCH
-)
+BYTES = 4 * (TOKENS * OUTCH + TOKENS * INCH + OUTCH * INCH) + 2 * (TOKENS * OUTCH + TOKENS * INCH + OUTCH * INCH)
 
 F32 = mybir.dt.float32
 BF16 = mybir.dt.bfloat16
@@ -19,22 +17,114 @@ ALU = mybir.AluOpType
 ACT = mybir.ActivationFunctionType
 
 P = 128
-K_PASS = 512
+PACK = 4
+K_PASS = P * PACK
 N_TILE = 512
 GROUPS = TOKENS // K_PASS
 CHUNKS = OUTCH // K_PASS
 HALVES = INCH // N_TILE
-UNITS = GROUPS * CHUNKS
-STEPS = 2 * UNITS
+
+STEPS = 2 * GROUPS * CHUNKS
+LAST = STEPS - 1
 
 H = 2.0**-7
-CLAMP = 9.0
 OFFSETS = (H, -H, 2.0 * H, -2.0 * H)
+CLAMP = 9.0
+
+TENSOR_TILES, TENSOR_RANGE = 12, 20
+
+DEPTH = {
+    "pre": 4,
+    "grad": 3,
+    "gel0": 3,
+    "gel1": 3,
+    "gel2": 3,
+    "gel3": 3,
+    "dz": 5,
+    "dz_tok": 2,
+    "dz_fea": 3,
+    "raw": 3,
+    "raw_i": 2,
+    "stage": 4,
+    "sum": 2,
+    "words": 2,
+    "acc": 4,
+}
+
+START = 10
+MATMUL_F32, MATMUL_MX, TRANSPOSE = 1120, 290, 80
+WEAVE = {"vector": 0.58, "scalar": 1.0}
+BUS = 0.28
+DMA_ISSUE, DMA_LEAD, DMA_TAIL = 70, 700, 1200
+HANDOVER = 260
+NEVER = 1e18
+
+PRE_LEAD, CLAMP_LEAD = 5, 9
+GRAD_LAG = 7
+URGENT = 20
+DW_LEAD = 12
+COPY_LEAD = 25
+VECTOR_SHARE, LATE_VECTOR_SHARE = 10, 3
 
 
-def tile_loratacmlp4_pb_v_kernel(
-    tc, h, z, u, b, W_out, b_out, pre, grad_out, out_0, out_1
-):
+def plan(tasks):
+    number = {}
+    for i in range(len(tasks)):
+        number[tasks[i][0]] = i
+    waits = [len(task[4]) for task in tasks]
+    followers = [[] for task in tasks]
+    users = {}
+    for i in range(len(tasks)):
+        for name in tasks[i][4]:
+            followers[number[name]].append(i)
+        for tile in tasks[i][5]:
+            users[tile] = users.get(tile, 0) + 1
+    ready = [0.0 for task in tasks]
+    clock = {"tensor": 0.0, "vector": 0.0, "scalar": 0.0, "sync": 0.0, "bus": 0.0}
+    places = {}
+    for kind in DEPTH:
+        places[kind] = [0.0 for i in range(DEPTH[kind])]
+    alive_until = {}
+    waiting = [i for i in range(len(tasks)) if waits[i] == 0]
+    planned = []
+    while waiting:
+        best = None
+        for i in waiting:
+            start = max(ready[i], clock[tasks[i][1]])
+            for tile in tasks[i][5]:
+                if tile not in alive_until:
+                    free = places[tile[0]]
+                    start = max(start, min(free) if free else NEVER)
+            if best is None or (start, tasks[i][3], i) < best:
+                best = (start, tasks[i][3], i)
+        start, urgency, i = best
+        assert start < NEVER
+        engine, work, tiles = tasks[i][1], tasks[i][2], tasks[i][5]
+        waiting.remove(i)
+        planned.append(tasks[i])
+        if engine == "sync":
+            clock["sync"] = start + DMA_ISSUE
+            clock["bus"] = max(start + DMA_LEAD, clock["bus"]) + work
+            end = clock["bus"] + DMA_TAIL
+        else:
+            end = clock[engine] = start + work
+        for tile in tiles:
+            if tile not in alive_until:
+                places[tile[0]].remove(min(places[tile[0]]))
+                alive_until[tile] = 0.0
+            alive_until[tile] = max(alive_until[tile], end)
+            users[tile] -= 1
+            if users[tile] == 0:
+                places[tile[0]].append(alive_until[tile] + HANDOVER)
+        for j in followers[i]:
+            ready[j] = max(ready[j], end if engine == "sync" else end + HANDOVER)
+            waits[j] -= 1
+            if waits[j] == 0:
+                waiting.append(j)
+    return planned
+
+
+def tile_loratacmlp4_pb_v_kernel(tc, h, z, u, b, W_out, b_out, pre, grad_out, out_0, out_1):
     nc = tc.nc
     h_rows = h.flatten_outer_dims()
     pre_rows = pre.flatten_outer_dims()
@@ -43,256 +133,338 @@ def tile_loratacmlp4_pb_v_kernel(
 
     with ExitStack() as ctx:
         keep = ctx.enter_context(tc.tile_pool(name="keep", bufs=1))
-        work = ctx.enter_context(tc.tile_pool(name="work", bufs=2))
+        pool = ctx.enter_context(tc.tile_pool(name="work", bufs=2))
         psum = ctx.enter_context(tc.psum_pool(name="psum", bufs=2))
+        ctx.enter_context(tc.manual_schedule())
 
-        offs = keep.tile([P, 4], F32, name="offs")
+        offsets = keep.tile([P, 4], F32, name="offsets")
         for k in range(4):
-            nc.vector.memset(offs[:, k : k + 1], OFFSETS[k])
+            nc.vector.memset(offsets[:, k : k + 1], OFFSETS[k])
         warm = keep.tile([P, 1], F32, name="warm")
-        nc.scalar.activation(out=warm[:], in_=offs[:, 0:1], func=ACT.Gelu, bias=offs[:, 0:1], scale=1.0)
-        ident = keep.tile([P, P], F32, name="ident")
-        make_identity(nc, ident[:])
+        nc.scalar.activation(out=warm[:], in_=offsets[:, 0:1], func=ACT.Gelu, bias=offsets[:, 0:1], scale=1.0)
+
+        identity = keep.tile([P, P], F32, name="identity")
+        make_identity(nc, identity[:])
+        scaled = keep.tile([P, 3, P], F32, name="scaled")
+        for k, weight in enumerate((8.0, -8.0, -1.0)):
+            nc.vector.tensor_scalar(out=scaled[:, k, :], in0=identity[:], scalar1=weight, scalar2=None, op0=ALU.mult)
+        weights = (scaled[:, 0, :], scaled[:, 1, :], scaled[:, 2, :], identity[:])
 
         w_codes = keep.tile([P, CHUNKS, INCH], U32, name="w_codes", align_bytes=64)
         w_scales = keep.tile([P, CHUNKS, INCH], U8, name="w_scales", align_bytes=64)
         h_codes = keep.tile([P, GROUPS, INCH], U32, name="h_codes", align_bytes=64)
         h_scales = keep.tile([P, GROUPS, INCH], U8, name="h_scales", align_bytes=64)
-        tok_codes = keep.tile([P, UNITS, K_PASS], U32, name="tok_codes", align_bytes=64)
-        tok_scales = keep.tile([P, UNITS, K_PASS], U8, name="tok_scales", align_bytes=64)
-        fea_codes = keep.tile([P, UNITS, K_PASS], U32, name="fea_codes", align_bytes=64)
-        fea_scales = keep.tile([P, UNITS, K_PASS], U8, name="fea_scales", align_bytes=64)
+        tok_codes = keep.tile([P, GROUPS, CHUNKS, K_PASS], U32, name="tok_codes", align_bytes=64)
+        tok_scales = keep.tile([P, GROUPS, CHUNKS, K_PASS], U8, name="tok_scales", align_bytes=64)
+        fea_codes = keep.tile([P, GROUPS, CHUNKS, K_PASS], U32, name="fea_codes", align_bytes=64)
+        fea_scales = keep.tile([P, GROUPS, CHUNKS, K_PASS], U8, name="fea_scales", align_bytes=64)
 
-        pre_t, grad_t, t_bank, gel, y_t, m_bank, dz_t = {}, {}, {}, {}, {}, {}, {}
+        order = [(0, c, half) for c in range(CHUNKS) for half in range(2)]
+        order += [(1, 0, half) for half in range(2)]
+        order += [(1, c, half) for half in range(2) for c in range(1, CHUNKS)]
+        step_of = {}
+        for s in range(STEPS):
+            step_of[order[s]] = s
+        last_chunk = order[LAST][1]
 
-        def where(s):
-            unit = s // 2
-            return unit // CHUNKS, unit % CHUNKS, s % 2
+        t = {}
 
-        def load_step(s):
-            if s >= STEPS:
-                return
-            g, c, half = where(s)
-            rows = slice(g * K_PASS, (g + 1) * K_PASS)
-            cols = slice(c * K_PASS, (c + 1) * K_PASS)
-            pre_t[s] = work.tile([P, 2, K_PASS], F32, name="pre_t", bufs=4)
-            nc.sync.dma_start(
-                out=pre_t[s][:],
-                in_=pre_rows[rows, cols].rearrange("(p j) w -> p j w", j=4)[:, 2 * half : 2 * half + 2, :],
+        def rows(g):
+            return slice(g * K_PASS, (g + 1) * K_PASS)
+
+        def load_pre(s, a, e):
+            g, c, half = order[s]
+            hbm = pre_rows[rows(g), rows(c)].rearrange("(p j) w -> p j w", j=PACK)
+            if a == 0:
+                t["pre", s] = pool.tile([P, 2, K_PASS], F32, name="pre", bufs=DEPTH["pre"])
+            nc.sync.dma_start(out=t["pre", s][:, a:e, :], in_=hbm[:, 2 * half + a : 2 * half + e, :])
+
+        def load_grad(g, pair):
+            hbm = grad_rows[rows(g), pair * 2 * K_PASS : (pair + 1) * 2 * K_PASS]
+            t["grad", g, pair] = pool.tile([P, PACK, 2 * K_PASS], BF16, name="grad", bufs=DEPTH["grad"])
+            nc.sync.dma_start(out=t["grad", g, pair][:], in_=hbm.rearrange("(p j) w -> p j w", j=PACK))
+
+        def clamp(s, a, e):
+            part = t["pre", s][:, a:e, :]
+            nc.vector.tensor_scalar(out=part, in0=part, scalar1=CLAMP, scalar2=-CLAMP, op0=ALU.min, op1=ALU.max)
+
+        def gelu(s, a, e, k):
+            name = "gel%d" % k
+            if a == 0:
+                t[name, s] = pool.tile([P, 2, K_PASS], F32, name=name, bufs=DEPTH[name])
+            nc.scalar.activation(
+                out=t[name, s][:, a:e, :],
+                in_=t["pre", s][:, a:e, :],
+                func=ACT.Gelu,
+                bias=offsets[:, k : k + 1],
+                scale=1.0,
             )
-            if half == 0:
-                grad_t[s // 2] = work.tile([P, 4, K_PASS], BF16, name="grad_t", bufs=3)
-                nc.sync.dma_start(
-                    out=grad_t[s // 2][:],
-                    in_=grad_rows[rows, cols].rearrange("(p j) w -> p j w", j=4),
-                )
 
-        def clamp_step(s):
-            if s < STEPS:
-                nc.gpsimd.tensor_scalar(
-                    out=pre_t[s][:], in0=pre_t[s][:], scalar1=CLAMP, scalar2=-CLAMP, op0=ALU.min, op1=ALU.max
-                )
+        def subtract(s, a, e, left, right):
+            out = t[left, s][:, a:e, :]
+            nc.vector.tensor_tensor(out=out, in0=out, in1=t[right, s][:, a:e, :], op=ALU.subtract)
 
-        def transpose_in(s, bk):
-            bank = psum.tile([P, 4, P], F32, name="t_bank", bufs=2)
-            t_bank[s, bk] = bank
-            for fb in range(4):
-                nc.tensor.transpose(bank[:, fb, :], pre_t[s][:, bk, fb * P : (fb + 1) * P], ident[:])
+        def join(s, a, e):
+            near, far = t["gel0", s][:, a:e, :], t["gel3", s][:, a:e, :]
+            nc.vector.scalar_tensor_tensor(out=near, in0=near, scalar=8.0, in1=far, op0=ALU.mult, op1=ALU.add)
 
-        def gelus(s, bk):
-            if bk == 0:
-                gel[s] = [work.tile([P, 2, K_PASS], F32, name="gel%d" % k, bufs=2) for k in range(4)]
+        def add_on_tensor(s, j):
+            t["sum", s, j] = psum.tile([P, K_PASS], F32, name="sum", bufs=DEPTH["sum"])
             for k in range(4):
-                nc.scalar.activation(
-                    out=gel[s][k][:, bk, :],
-                    in_=t_bank[s, bk][:].rearrange("p f q -> p (f q)"),
-                    func=ACT.Gelu,
-                    bias=offs[:, k : k + 1],
-                    scale=1.0,
+                nc.tensor.matmul(
+                    t["sum", s, j][:],
+                    lhsT=weights[k],
+                    rhs=t["gel%d" % k, s][:, j, :],
+                    start=(k == 0),
+                    stop=(k == 3),
                 )
 
-        def stencil(s):
-            gp1, gm1, gp2, gm2 = gel[s]
-            y1 = work.tile([P, 2, K_PASS], F32, name="y1", bufs=2)
-            y2 = work.tile([P, 2, K_PASS], F32, name="y2", bufs=2)
+        def finish(s, a, e, source):
+            g, c, half = order[s]
+            if ("dz", g, c) not in t:
+                t["dz", g, c] = pool.tile([P, PACK * K_PASS], BF16, name="dz", bufs=DEPTH["dz"], align_bytes=64)
+            j = slice(2 * half + a, 2 * half + e)
+            if source == "sum":
+                total = t["sum", s, a][:].rearrange("p (j w) -> p j w", j=1)
+            else:
+                total = t["gel0", s][:, a:e, :]
             nc.vector.scalar_tensor_tensor(
-                out=y1[:], in0=gp1[:], scalar=8.0, in1=gp2[:], op0=ALU.mult, op1=ALU.subtract
-            )
-            nc.vector.scalar_tensor_tensor(
-                out=y2[:], in0=gm1[:], scalar=-8.0, in1=gm2[:], op0=ALU.mult, op1=ALU.add
-            )
-            y_t[s] = (y1, y2)
-
-        def combine(s, bk):
-            bank = psum.tile([P, K_PASS], F32, name="m_bank", bufs=2)
-            m_bank[s, bk] = bank
-            y1, y2 = y_t[s]
-            for fb in range(4):
-                cols = slice(fb * P, (fb + 1) * P)
-                nc.tensor.matmul(bank[:, cols], lhsT=y1[:, bk, cols], rhs=ident[:], start=True, stop=False, is_transpose=True)
-                nc.tensor.matmul(bank[:, cols], lhsT=y2[:, bk, cols], rhs=ident[:], start=False, stop=True, is_transpose=True)
-
-        def finish(s, bk):
-            unit, j = s // 2, 2 * (s % 2) + bk
-            if j == 0:
-                dz_t[unit] = work.tile([P, 4 * K_PASS], BF16, name="dz_t", bufs=2, align_bytes=64)
-            nc.vector.scalar_tensor_tensor(
-                out=dz_t[unit][:, j * K_PASS : (j + 1) * K_PASS],
-                in0=m_bank[s, bk][:],
+                out=t["dz", g, c][:].rearrange("p (j w) -> p j w", j=PACK)[:, j, :],
+                in0=total,
                 scalar=1.0 / (12.0 * H),
-                in1=grad_t[unit][:, j, :],
+                in1=t["grad", g, c // 2][:, j, rows(c % 2)],
                 op0=ALU.mult,
                 op1=ALU.mult,
             )
 
-        pending_quant = []
-
-        def interleave_tokens(unit):
-            dst = work.tile([P, 4 * K_PASS], BF16, name="dz_tok", bufs=2, align_bytes=64)
+        def weave_tokens(g, c, f0, f1):
+            woven = pool.tile([P, PACK * (f1 - f0)], BF16, name="dz_tok", bufs=DEPTH["dz_tok"], align_bytes=64)
+            t["dz_tok", g, c, f0] = woven
+            dz = t["dz", g, c][:].rearrange("p (j w) -> p j w", j=PACK)[:, :, f0:f1]
             nc.vector.tensor_copy(
-                out=dst[:].rearrange("p (c i t) -> p c t i", i=4, t=4),
-                in_=dz_t[unit][:].rearrange("p (t c i) -> p c t i", i=4, t=4),
-            )
-            pending_quant.append(
-                lambda: nc.vector.quantize_mx(
-                    out=tok_codes[:, unit, :].bitcast(E5M2), scales=tok_scales[:, unit, :], in_=dst[:]
-                )
+                out=woven[:].rearrange("p (w i j) -> p w j i", i=4, j=PACK),
+                in_=dz.rearrange("p j (w i) -> p w j i", i=4),
             )
 
-        def transpose_words(unit):
-            words = dz_t[unit][:].bitcast(F32)
-            dst = work.tile([P, 4 * K_PASS], BF16, name="dz_fea", bufs=2, align_bytes=64)
-            dst_words = dst[:].bitcast(F32).rearrange("p (j r u) -> p j r u", j=4, u=2)
-            for jp in range(2):
-                bank = psum.tile([P, 2, 2, P], F32, name="w_bank", bufs=1)
-                for j in range(2):
-                    base = (2 * jp + j) * (K_PASS // 2)
-                    for e in range(2):
-                        nc.tensor.transpose(bank[:, j, e, :], words[:, base + e : base + K_PASS // 2 : 2], ident[:])
-                nc.scalar.copy(
-                    out=dst_words[:, 2 * jp : 2 * jp + 2, :, :], in_=bank[:].rearrange("p j u r -> p j r u")
-                )
-            pending_quant.append(
-                lambda: nc.vector.quantize_mx(
-                    out=fea_codes[:, unit, :].bitcast(E5M2), scales=fea_scales[:, unit, :], in_=dst[:]
-                )
+        def quantize_tokens(g, c, f0, f1):
+            nc.vector.quantize_mx(
+                out=tok_codes[:, g, c, f0:f1].bitcast(E5M2),
+                scales=tok_scales[:, g, c, f0:f1],
+                in_=t["dz_tok", g, c, f0][:],
             )
 
-        raw_t = {}
+        def transpose_words(s):
+            g, c, half = order[s]
+            words = t["dz", g, c][:].bitcast(F32)
+            t["words", s] = psum.tile([P, 2, 2, P], F32, name="words", bufs=DEPTH["words"])
+            for j in range(2):
+                first = (2 * half + j) * (K_PASS // 2)
+                for e in range(2):
+                    pairs = words[:, first + e : first + K_PASS // 2 : 2]
+                    nc.tensor.transpose(t["words", s][:, j, e, :], pairs, identity[:])
 
-        def load_raw(kind, i):
-            src = W_out if kind == "w" else h_rows
-            raw = work.tile([P, 4, INCH], BF16, name="raw", bufs=2)
-            nc.sync.dma_start(
-                out=raw[:], in_=src[i * K_PASS : (i + 1) * K_PASS, :].rearrange("(p j) n -> p j n", j=4)
+        def copy_words(s):
+            woven = pool.tile([P, 2 * K_PASS], BF16, name="dz_fea", bufs=DEPTH["dz_fea"], align_bytes=64)
+            t["dz_fea", s] = woven
+            nc.scalar.copy(
+                out=woven[:].bitcast(F32).rearrange("p (j q e) -> p j q e", j=2, e=2),
+                in_=t["words", s][:].rearrange("p j e q -> p j q e"),
             )
-            raw_t[kind, i] = raw
 
-        def interleave_raw(kind, i, engine):
-            raw = raw_t[kind, i]
-            dst = work.tile([P, 4 * INCH], BF16, name="raw_i", bufs=2, align_bytes=64)
-            move = nc.vector.tensor_copy if engine == "v" else nc.scalar.copy
+        def quantize_features(s):
+            g, c, half = order[s]
+            cols = slice(half * 2 * P, (half + 1) * 2 * P)
+            nc.vector.quantize_mx(
+                out=fea_codes[:, g, c, cols].bitcast(E5M2), scales=fea_scales[:, g, c, cols], in_=t["dz_fea", s][:]
+            )
+
+        def load_operand(which, k, n):
+            source = W_out if which == "w" else h_rows
+            hbm = source[rows(k), n * N_TILE : (n + 1) * N_TILE]
+            t["raw", which, k, n] = pool.tile([P, PACK, N_TILE], BF16, name="raw", bufs=DEPTH["raw"])
+            nc.sync.dma_start(out=t["raw", which, k, n][:], in_=hbm.rearrange("(p j) n -> p j n", j=PACK))
+
+        def weave_operand(which, k, n, engine):
+            woven = pool.tile([P, PACK * N_TILE], BF16, name="raw_i", bufs=DEPTH["raw_i"], align_bytes=64)
+            t["raw_i", which, k, n] = woven
+            move = nc.vector.tensor_copy if engine == "vector" else nc.scalar.copy
             move(
-                out=dst[:].rearrange("p (c i t) -> p c t i", i=4, t=4),
-                in_=raw[:].rearrange("p t (c i) -> p c t i", i=4),
-            )
-            codes, scales = (w_codes, w_scales) if kind == "w" else (h_codes, h_scales)
-            pending_quant.append(
-                lambda: nc.vector.quantize_mx(out=codes[:, i, :].bitcast(E4M3), scales=scales[:, i, :], in_=dst[:])
+                out=woven[:].rearrange("p (c i j) -> p c j i", i=4, j=PACK),
+                in_=t["raw", which, k, n][:].rearrange("p j (c i) -> p c j i", i=4),
             )
 
-        ready, evacs = [], []
-        stage = {}
+        def quantize_operand(which, k, n):
+            codes, scales = (w_codes, w_scales) if which == "w" else (h_codes, h_scales)
+            cols = slice(n * N_TILE, (n + 1) * N_TILE)
+            nc.vector.quantize_mx(
+                out=codes[:, k, cols].bitcast(E4M3), scales=scales[:, k, cols], in_=t["raw_i", which, k, n][:]
+            )
 
-        def mx_group(kind, row, m, n):
-            acc = psum.tile([P, N_TILE], F32, name="acc", bufs=3)
+        def multiply(which, row, m, n):
+            acc = psum.tile([P, N_TILE], F32, name="acc", bufs=DEPTH["acc"])
+            t["acc", which, row, m, n] = acc
+            passes = CHUNKS if which == "dh" else GROUPS
             m_cols = slice(m * P, (m + 1) * P)
             n_cols = slice(n * N_TILE, (n + 1) * N_TILE)
-            passes = CHUNKS if kind == "dh" else GROUPS
             for k in range(passes):
-                if kind == "dh":
-                    unit = row * CHUNKS + k
-                    lc, ls, rc, rs = fea_codes, fea_scales, w_codes, w_scales
+                if which == "dh":
+                    dz_codes, dz_scales = fea_codes[:, row, k, m_cols], fea_scales[:, row, k, m_cols]
+                    codes, scales = w_codes[:, k, n_cols], w_scales[:, k, n_cols]
                 else:
-                    unit = k * CHUNKS + row
-                    lc, ls, rc, rs = tok_codes, tok_scales, h_codes, h_scales
+                    dz_codes, dz_scales = tok_codes[:, k, row, m_cols], tok_scales[:, k, row, m_cols]
+                    codes, scales = h_codes[:, k, n_cols], h_scales[:, k, n_cols]
                 nc.tensor.matmul_mx(
                     out=acc[:],
-                    lhsT=lc[:, unit, m_cols].bitcast(E5M2),
-                    lhsT_scale=ls[:, unit, m_cols],
-                    rhs=rc[:, k, n_cols].bitcast(E4M3),
-                    rhs_scale=rs[:, k, n_cols],
+                    lhsT=dz_codes.bitcast(E5M2),
+                    lhsT_scale=dz_scales,
+                    rhs=codes.bitcast(E4M3),
+                    rhs_scale=scales,
                     start=(k == 0),
                     stop=(k == passes - 1),
                 )
-            evacs.append((kind, row, m, n, acc))
 
-        def evacuate(kind, row, m, n, acc):
-            n_cols = slice(n * N_TILE, (n + 1) * N_TILE)
-            if n == 0:
-                stage[kind, row, m] = work.tile([P, INCH], F32, name="stage", bufs=4)
-            dst = stage[kind, row, m]
-            if n == 0:
-                nc.scalar.copy(out=dst[:, n_cols], in_=acc[:])
+        def copy_out(which, row, m, n, engine):
+            if ("stage", which, row, m) not in t:
+                t["stage", which, row, m] = pool.tile([P, INCH], F32, name="stage", bufs=DEPTH["stage"])
+            move = nc.vector.tensor_copy if engine == "vector" else nc.scalar.copy
+            move(
+                out=t["stage", which, row, m][:, n * N_TILE : (n + 1) * N_TILE],
+                in_=t["acc", which, row, m, n][:],
+            )
+
+        def store(which, row, m, c0, c1):
+            if which == "dh":
+                hbm = dh_rows[rows(row), c0:c1].rearrange("(p j) n -> p j n", j=PACK)[:, m, :]
             else:
-                nc.vector.tensor_copy(out=dst[:, n_cols], in_=acc[:])
-            if n == HALVES - 1:
-                if kind == "dh":
-                    hbm = dh_rows[row * K_PASS : (row + 1) * K_PASS, :].rearrange("(p j) n -> p j n", j=4)[:, m, :]
-                else:
-                    hbm = out_1[row * K_PASS + m * P : row * K_PASS + (m + 1) * P, :]
-                nc.sync.dma_start(out=hbm, in_=dst[:])
+                first = row * K_PASS + m * P
+                hbm = out_1[first : first + P, c0:c1]
+            nc.sync.dma_start(out=hbm, in_=t["stage", which, row, m][:, c0:c1])
 
-        def drain_mx(count):
-            for e in list(evacs):
-                evacuate(*e)
-            evacs.clear()
-            for i in range(min(count, len(ready))):
-                mx_group(*ready[i])
-            for i in range(min(count, len(ready))):
-                ready.remove(ready[0])
+        tasks = []
 
-        fills = [("w", 0), ("w", 1), ("w", 2), ("w", 3), ("h", 0), ("h", 1)]
-        engines = ["v", "s", "v", "s", "v", "v"]
+        def task(name, engine, work, urgency, after, tiles, emit, *args):
+            tasks.append((name, engine, work, urgency, after, tiles, lambda: emit(*args)))
 
-        for s in range(3):
-            load_step(s)
-        load_raw(*fills[0])
-        clamp_step(0)
-        step = 0
-        while step < STEPS + 4 or ready or evacs:
-            load_step(step + 3)
-            if step % 2 == 0 and step // 2 + 1 < len(fills):
-                load_raw(*fills[step // 2 + 1])
-            if step < STEPS:
-                clamp_step(step + 1)
-            new_ready = []
-            quants = list(pending_quant)
-            pending_quant.clear()
-            for bk in range(2):
-                if step < STEPS:
-                    transpose_in(step, bk)
-                    gelus(step, bk)
-                if 0 <= step - 2 < STEPS:
-                    combine(step - 2, bk)
-                    finish(step - 2, bk)
-                drain_mx(3)
-            if 0 <= step - 1 < STEPS:
-                stencil(step - 1)
-            for q in quants:
-                q()
-            if 0 <= step - 3 < STEPS and (step - 3) % 2 == 1:
-                unit = (step - 3) // 2
-                g, c = unit // CHUNKS, unit % CHUNKS
-                if c == CHUNKS - 1:
-                    new_ready += [("dh", g, m, n) for m in range(4) for n in range(HALVES)]
-                if g == GROUPS - 1:
-                    new_ready += [("dw", c, m, n) for m in range(4) for n in range(HALVES)]
-            ready += new_ready
-            if 0 <= step - 2 < STEPS and (step - 2) % 2 == 1:
-                unit = (step - 2) // 2
-                interleave_tokens(unit)
-                transpose_words(unit)
-            if step % 2 == 1 and step // 2 < len(fills):
-                interleave_raw(*fills[step // 2], engines[step // 2])
-            step += 1
+        def columns(n):
+            return START + n
+
+        for q in range(GROUPS * CHUNKS // 2):
+            g, pair = q // 2, q % 2
+            work = BUS * 2 * PACK * 2 * K_PASS
+            task(("grad", g, pair), "sync", work, 4 * q + GRAD_LAG, [], [("grad", g, pair)], load_grad, g, pair)
+
+        finished = {}
+        for s in range(STEPS):
+            g, c, half = order[s]
+            parts = ((0, 1), (1, 2)) if s in (0, LAST) else ((0, 2),)
+            for a, e in parts if s == 0 else ((0, 2),):
+                n = (e - a) * K_PASS
+                tile = [("pre", s)]
+                task(("load", s, a), "sync", BUS * 4 * n, s - PRE_LEAD, [], tile, load_pre, s, a, e)
+                work, after = columns(n / 2), [("load", s, a)]
+                task(("clamp", s, a), "vector", work, s - CLAMP_LEAD, after, tile, clamp, s, a, e)
+            for a, e in parts:
+                work, after = columns((e - a) * K_PASS), [("clamp", s, a if s == 0 else 0)]
+                for k in range(4):
+                    tiles = [("pre", s), ("gel%d" % k, s)]
+                    task(("gelu", s, a, k), "scalar", work, s, after, tiles, gelu, s, a, e, k)
+
+            def value(a, k):
+                return ("gelu", s, a if len(parts) == 2 else 0, k)
+
+            on_tensor = []
+            for j in range(2):
+                i = 2 * s + j
+                if i < TENSOR_RANGE and (i + 1) * TENSOR_TILES // TENSOR_RANGE > i * TENSOR_TILES // TENSOR_RANGE:
+                    on_tensor.append(j)
+            if not on_tensor:
+                vector_parts = parts
+            else:
+                vector_parts = [(j, j + 1) for j in range(2) if j not in on_tensor]
+            done = []
+            grad, dz_tiles = ("grad", g, c // 2), [("dz", g, c), ("grad", g, c // 2)]
+            for j in on_tensor:
+                after = [value(j, k) for k in range(4)]
+                tiles = [("gel%d" % k, s) for k in range(4)] + [("sum", s, j)]
+                task(("add", s, j), "tensor", 4 * MATMUL_F32, s, after, tiles, add_on_tensor, s, j)
+                after, tiles = [("add", s, j), grad], dz_tiles + [("sum", s, j)]
+                task(("dz", s, j), "vector", columns(K_PASS), s - URGENT, after, tiles, finish, s, j, j + 1, "sum")
+                done.append(("dz", s, j))
+            for a, e in vector_parts:
+                work = columns((e - a) * K_PASS)
+                after, tiles = [value(a, 0), value(a, 1)], [("gel0", s), ("gel1", s)]
+                task(("near", s, a), "vector", work, s, after, tiles, subtract, s, a, e, "gel0", "gel1")
+                after, tiles = [value(a, 2), value(a, 3)], [("gel2", s), ("gel3", s)]
+                task(("far", s, a), "vector", work, s, after, tiles, subtract, s, a, e, "gel3", "gel2")
+                after, tiles = [("near", s, a), ("far", s, a)], [("gel0", s), ("gel3", s)]
+                task(("join", s, a), "vector", work, s, after, tiles, join, s, a, e)
+                after, tiles = [("join", s, a), grad], dz_tiles + [("gel0", s)]
+                task(("dz", s, a), "vector", work, s - URGENT, after, tiles, finish, s, a, e, "gel0")
+                done.append(("dz", s, a))
+            finished[s] = done
+
+            tiles = [("words", s), ("dz", g, c)]
+            task(("words", s), "tensor", 4 * TRANSPOSE, s, done, tiles, transpose_words, s)
+            tiles = [("words", s), ("dz_fea", s)]
+            task(("copy", s), "scalar", columns(K_PASS), s, [("words", s)], tiles, copy_words, s)
+            tiles = [("dz_fea", s)]
+            task(("features", s), "vector", columns(K_PASS / 2), s, [("copy", s)], tiles, quantize_features, s)
+            if half == 1:
+                width = K_PASS // 2 if s == LAST else K_PASS
+                for f0 in range(0, K_PASS, width):
+                    f1 = f0 + width
+                    work, after = columns(WEAVE["vector"] * PACK * width), finished[step_of[g, c, 0]] + done
+                    tiles = [("dz", g, c), ("dz_tok", g, c, f0)]
+                    task(("weave", g, c, f0), "vector", work, s - URGENT, after, tiles, weave_tokens, g, c, f0, f1)
+                    work, after, tiles = columns(width), [("weave", g, c, f0)], [("dz_tok", g, c, f0)]
+                    task(("tokens", g, c, f0), "vector", work, s - URGENT, after, tiles, quantize_tokens, g, c, f0, f1)
+
+        operands = [("w", k, n) for k in range(CHUNKS) for n in range(HALVES)]
+        operands += [("h", k, n) for k in range(GROUPS) for n in range(HALVES)]
+        for i in range(len(operands)):
+            which, k, n = operands[i]
+            urgency = 11 - i / 2 if which == "w" else 20 + 5 * (i - CHUNKS * HALVES)
+            engine = "scalar" if i in (1, 3) else "vector"
+            size, raw, woven = PACK * N_TILE, ("raw", which, k, n), ("raw_i", which, k, n)
+            early = urgency - 1 if i > 0 else -5.0
+            task(("load", which, k, n), "sync", BUS * 2 * size, early, [], [raw], load_operand, which, k, n)
+            work, after = columns(WEAVE[engine] * size), [("load", which, k, n)]
+            task(("weave", which, k, n), engine, work, urgency, after, [raw, woven], weave_operand, which, k, n, engine)
+            work, after = columns(size / 4), [("weave", which, k, n)]
+            task(("quantize", which, k, n), "vector", work, urgency + 1, after, [woven], quantize_operand, which, k, n)
+
+        products = []
+        for g in range(GROUPS):
+            for m in range(PACK):
+                steps = [step_of[g, c, m // 2] for c in range(CHUNKS)]
+                for n in range(HALVES):
+                    after = [("features", s) for s in steps] + [("quantize", "w", k, n) for k in range(CHUNKS)]
+                    products.append((max(steps) - URGENT, "dh", g, m, n, after))
+        for c in range(CHUNKS):
+            for m in range(K_PASS // P):
+                f0 = m // 2 * (K_PASS // 2) if c == last_chunk else 0
+                for n in range(HALVES):
+                    after = [("tokens", 0, c, 0), ("tokens", 1, c, f0)]
+                    after += [("quantize", "h", k, n) for k in range(GROUPS)]
+                    products.append((step_of[1, c, 1] - DW_LEAD, "dw", c, m, n, after))
+        products = sorted(products, key=lambda product: product[:5])
+        for i in range(len(products)):
+            urgency, which, row, m, n, after = products[i]
+            late = row == last_chunk if which == "dw" else row == 1 and m >= 2
+            share = LATE_VECTOR_SHARE if late else VECTOR_SHARE
+            engine = "vector" if i % share == share - 1 else "scalar"
+            acc, stage = ("acc", which, row, m, n), ("stage", which, row, m)
+            work = (CHUNKS if which == "dh" else GROUPS) * MATMUL_MX
+            task(("multiply", which, row, m, n), "tensor", work, urgency, after, [acc], multiply, which, row, m, n)
+            work, after = columns(N_TILE), [("multiply", which, row, m, n)]
+            early = urgency - COPY_LEAD
+            task(("out", which, row, m, n), engine, work, early, after, [acc, stage], copy_out, which, row, m, n, engine)
+            if late:
+                work, after, cols = BUS * 4 * N_TILE, [("out", which, row, m, n)], (n * N_TILE, (n + 1) * N_TILE)
+            elif n == HALVES - 1:
+                work, after, cols = BUS * 4 * INCH, [("out", which, row, m, i) for i in range(HALVES)], (0, INCH)
+            if late or n == HALVES - 1:
+                task(("store", which, row, m, n), "sync", work, urgency, after, [stage], store, which, row, m, *cols)
+
+        for planned in plan(tasks):
+            planned[6]()

from contextlib import ExitStack

import concourse.mybir as mybir
from concourse.masks import make_identity

TOKENS, OUTCH, INCH = 1024, 2048, 1024
FLOPS = 2 * 2 * TOKENS * OUTCH * INCH
BYTES = 4 * (TOKENS * OUTCH + TOKENS * INCH + OUTCH * INCH) + 2 * (TOKENS * OUTCH + TOKENS * INCH + OUTCH * INCH)

F32 = mybir.dt.float32
BF16 = mybir.dt.bfloat16
U32 = mybir.dt.uint32
U8 = mybir.dt.uint8
E4M3 = mybir.dt.float8_e4m3fn_x4
E5M2 = mybir.dt.float8_e5m2_x4
ALU = mybir.AluOpType
ACT = mybir.ActivationFunctionType

P = 128
PACK = 4
K_PASS = P * PACK
N_TILE = 512
GROUPS = TOKENS // K_PASS
CHUNKS = OUTCH // K_PASS
HALVES = INCH // N_TILE

STEPS = 2 * GROUPS * CHUNKS
LAST = STEPS - 1

H = 2.0**-7
OFFSETS = (H, -H, 2.0 * H, -2.0 * H)
CLAMP = 9.0

TENSOR_TILES, TENSOR_RANGE = 12, 20

DEPTH = {
    "pre": 4,
    "grad": 3,
    "gel0": 3,
    "gel1": 3,
    "gel2": 3,
    "gel3": 3,
    "dz": 5,
    "dz_tok": 2,
    "dz_fea": 3,
    "raw": 3,
    "raw_i": 2,
    "stage": 4,
    "sum": 2,
    "words": 2,
    "acc": 4,
}

START = 10
MATMUL_F32, MATMUL_MX, TRANSPOSE = 1120, 290, 80
WEAVE = {"vector": 0.58, "scalar": 1.0}
BUS = 0.28
DMA_ISSUE, DMA_LEAD, DMA_TAIL = 70, 700, 1200
HANDOVER = 260
NEVER = 1e18

PRE_LEAD, CLAMP_LEAD = 5, 9
GRAD_LAG = 7
URGENT = 20
DW_LEAD = 12
COPY_LEAD = 25
VECTOR_SHARE, LATE_VECTOR_SHARE = 10, 3


def plan(tasks):
    number = {}
    for i in range(len(tasks)):
        number[tasks[i][0]] = i
    waits = [len(task[4]) for task in tasks]
    followers = [[] for task in tasks]
    users = {}
    for i in range(len(tasks)):
        for name in tasks[i][4]:
            followers[number[name]].append(i)
        for tile in tasks[i][5]:
            users[tile] = users.get(tile, 0) + 1
    ready = [0.0 for task in tasks]
    clock = {"tensor": 0.0, "vector": 0.0, "scalar": 0.0, "sync": 0.0, "bus": 0.0}
    places = {}
    for kind in DEPTH:
        places[kind] = [0.0 for i in range(DEPTH[kind])]
    alive_until = {}
    waiting = [i for i in range(len(tasks)) if waits[i] == 0]
    planned = []
    while waiting:
        best = None
        for i in waiting:
            start = max(ready[i], clock[tasks[i][1]])
            for tile in tasks[i][5]:
                if tile not in alive_until:
                    free = places[tile[0]]
                    start = max(start, min(free) if free else NEVER)
            if best is None or (start, tasks[i][3], i) < best:
                best = (start, tasks[i][3], i)
        start, urgency, i = best
        assert start < NEVER
        engine, work, tiles = tasks[i][1], tasks[i][2], tasks[i][5]
        waiting.remove(i)
        planned.append(tasks[i])
        if engine == "sync":
            clock["sync"] = start + DMA_ISSUE
            clock["bus"] = max(start + DMA_LEAD, clock["bus"]) + work
            end = clock["bus"] + DMA_TAIL
        else:
            end = clock[engine] = start + work
        for tile in tiles:
            if tile not in alive_until:
                places[tile[0]].remove(min(places[tile[0]]))
                alive_until[tile] = 0.0
            alive_until[tile] = max(alive_until[tile], end)
            users[tile] -= 1
            if users[tile] == 0:
                places[tile[0]].append(alive_until[tile] + HANDOVER)
        for j in followers[i]:
            ready[j] = max(ready[j], end if engine == "sync" else end + HANDOVER)
            waits[j] -= 1
            if waits[j] == 0:
                waiting.append(j)
    return planned


def tile_loratacmlp4_pb_v_kernel(tc, h, z, u, b, W_out, b_out, pre, grad_out, out_0, out_1):
    nc = tc.nc
    h_rows = h.flatten_outer_dims()
    pre_rows = pre.flatten_outer_dims()
    grad_rows = grad_out.flatten_outer_dims()
    dh_rows = out_0.flatten_outer_dims()

    with ExitStack() as ctx:
        keep = ctx.enter_context(tc.tile_pool(name="keep", bufs=1))
        pool = ctx.enter_context(tc.tile_pool(name="work", bufs=2))
        psum = ctx.enter_context(tc.psum_pool(name="psum", bufs=2))
        ctx.enter_context(tc.manual_schedule())

        offsets = keep.tile([P, 4], F32, name="offsets")
        for k in range(4):
            nc.vector.memset(offsets[:, k : k + 1], OFFSETS[k])
        warm = keep.tile([P, 1], F32, name="warm")
        nc.scalar.activation(out=warm[:], in_=offsets[:, 0:1], func=ACT.Gelu, bias=offsets[:, 0:1], scale=1.0)

        identity = keep.tile([P, P], F32, name="identity")
        make_identity(nc, identity[:])
        scaled = keep.tile([P, 3, P], F32, name="scaled")
        for k, weight in enumerate((8.0, -8.0, -1.0)):
            nc.vector.tensor_scalar(out=scaled[:, k, :], in0=identity[:], scalar1=weight, scalar2=None, op0=ALU.mult)
        weights = (scaled[:, 0, :], scaled[:, 1, :], scaled[:, 2, :], identity[:])

        w_codes = keep.tile([P, CHUNKS, INCH], U32, name="w_codes", align_bytes=64)
        w_scales = keep.tile([P, CHUNKS, INCH], U8, name="w_scales", align_bytes=64)
        h_codes = keep.tile([P, GROUPS, INCH], U32, name="h_codes", align_bytes=64)
        h_scales = keep.tile([P, GROUPS, INCH], U8, name="h_scales", align_bytes=64)
        tok_codes = keep.tile([P, GROUPS, CHUNKS, K_PASS], U32, name="tok_codes", align_bytes=64)
        tok_scales = keep.tile([P, GROUPS, CHUNKS, K_PASS], U8, name="tok_scales", align_bytes=64)
        fea_codes = keep.tile([P, GROUPS, CHUNKS, K_PASS], U32, name="fea_codes", align_bytes=64)
        fea_scales = keep.tile([P, GROUPS, CHUNKS, K_PASS], U8, name="fea_scales", align_bytes=64)

        order = [(0, c, half) for c in range(CHUNKS) for half in range(2)]
        order += [(1, 0, half) for half in range(2)]
        order += [(1, c, half) for half in range(2) for c in range(1, CHUNKS)]
        step_of = {}
        for s in range(STEPS):
            step_of[order[s]] = s
        last_chunk = order[LAST][1]

        t = {}

        def rows(g):
            return slice(g * K_PASS, (g + 1) * K_PASS)

        def load_pre(s, a, e):
            g, c, half = order[s]
            hbm = pre_rows[rows(g), rows(c)].rearrange("(p j) w -> p j w", j=PACK)
            if a == 0:
                t["pre", s] = pool.tile([P, 2, K_PASS], F32, name="pre", bufs=DEPTH["pre"])
            nc.sync.dma_start(out=t["pre", s][:, a:e, :], in_=hbm[:, 2 * half + a : 2 * half + e, :])

        def load_grad(g, pair):
            hbm = grad_rows[rows(g), pair * 2 * K_PASS : (pair + 1) * 2 * K_PASS]
            t["grad", g, pair] = pool.tile([P, PACK, 2 * K_PASS], BF16, name="grad", bufs=DEPTH["grad"])
            nc.sync.dma_start(out=t["grad", g, pair][:], in_=hbm.rearrange("(p j) w -> p j w", j=PACK))

        def clamp(s, a, e):
            part = t["pre", s][:, a:e, :]
            nc.vector.tensor_scalar(out=part, in0=part, scalar1=CLAMP, scalar2=-CLAMP, op0=ALU.min, op1=ALU.max)

        def gelu(s, a, e, k):
            name = "gel%d" % k
            if a == 0:
                t[name, s] = pool.tile([P, 2, K_PASS], F32, name=name, bufs=DEPTH[name])
            nc.scalar.activation(
                out=t[name, s][:, a:e, :],
                in_=t["pre", s][:, a:e, :],
                func=ACT.Gelu,
                bias=offsets[:, k : k + 1],
                scale=1.0,
            )

        def subtract(s, a, e, left, right):
            out = t[left, s][:, a:e, :]
            nc.vector.tensor_tensor(out=out, in0=out, in1=t[right, s][:, a:e, :], op=ALU.subtract)

        def join(s, a, e):
            near, far = t["gel0", s][:, a:e, :], t["gel3", s][:, a:e, :]
            nc.vector.scalar_tensor_tensor(out=near, in0=near, scalar=8.0, in1=far, op0=ALU.mult, op1=ALU.add)

        def add_on_tensor(s, j):
            t["sum", s, j] = psum.tile([P, K_PASS], F32, name="sum", bufs=DEPTH["sum"])
            for k in range(4):
                nc.tensor.matmul(
                    t["sum", s, j][:],
                    lhsT=weights[k],
                    rhs=t["gel%d" % k, s][:, j, :],
                    start=(k == 0),
                    stop=(k == 3),
                )

        def finish(s, a, e, source):
            g, c, half = order[s]
            if ("dz", g, c) not in t:
                t["dz", g, c] = pool.tile([P, PACK * K_PASS], BF16, name="dz", bufs=DEPTH["dz"], align_bytes=64)
            j = slice(2 * half + a, 2 * half + e)
            if source == "sum":
                total = t["sum", s, a][:].rearrange("p (j w) -> p j w", j=1)
            else:
                total = t["gel0", s][:, a:e, :]
            nc.vector.scalar_tensor_tensor(
                out=t["dz", g, c][:].rearrange("p (j w) -> p j w", j=PACK)[:, j, :],
                in0=total,
                scalar=1.0 / (12.0 * H),
                in1=t["grad", g, c // 2][:, j, rows(c % 2)],
                op0=ALU.mult,
                op1=ALU.mult,
            )

        def weave_tokens(g, c, f0, f1):
            woven = pool.tile([P, PACK * (f1 - f0)], BF16, name="dz_tok", bufs=DEPTH["dz_tok"], align_bytes=64)
            t["dz_tok", g, c, f0] = woven
            dz = t["dz", g, c][:].rearrange("p (j w) -> p j w", j=PACK)[:, :, f0:f1]
            nc.vector.tensor_copy(
                out=woven[:].rearrange("p (w i j) -> p w j i", i=4, j=PACK),
                in_=dz.rearrange("p j (w i) -> p w j i", i=4),
            )

        def quantize_tokens(g, c, f0, f1):
            nc.vector.quantize_mx(
                out=tok_codes[:, g, c, f0:f1].bitcast(E5M2),
                scales=tok_scales[:, g, c, f0:f1],
                in_=t["dz_tok", g, c, f0][:],
            )

        def transpose_words(s):
            g, c, half = order[s]
            words = t["dz", g, c][:].bitcast(F32)
            t["words", s] = psum.tile([P, 2, 2, P], F32, name="words", bufs=DEPTH["words"])
            for j in range(2):
                first = (2 * half + j) * (K_PASS // 2)
                for e in range(2):
                    pairs = words[:, first + e : first + K_PASS // 2 : 2]
                    nc.tensor.transpose(t["words", s][:, j, e, :], pairs, identity[:])

        def copy_words(s):
            woven = pool.tile([P, 2 * K_PASS], BF16, name="dz_fea", bufs=DEPTH["dz_fea"], align_bytes=64)
            t["dz_fea", s] = woven
            nc.scalar.copy(
                out=woven[:].bitcast(F32).rearrange("p (j q e) -> p j q e", j=2, e=2),
                in_=t["words", s][:].rearrange("p j e q -> p j q e"),
            )

        def quantize_features(s):
            g, c, half = order[s]
            cols = slice(half * 2 * P, (half + 1) * 2 * P)
            nc.vector.quantize_mx(
                out=fea_codes[:, g, c, cols].bitcast(E5M2), scales=fea_scales[:, g, c, cols], in_=t["dz_fea", s][:]
            )

        def load_operand(which, k, n):
            source = W_out if which == "w" else h_rows
            hbm = source[rows(k), n * N_TILE : (n + 1) * N_TILE]
            t["raw", which, k, n] = pool.tile([P, PACK, N_TILE], BF16, name="raw", bufs=DEPTH["raw"])
            nc.sync.dma_start(out=t["raw", which, k, n][:], in_=hbm.rearrange("(p j) n -> p j n", j=PACK))

        def weave_operand(which, k, n, engine):
            woven = pool.tile([P, PACK * N_TILE], BF16, name="raw_i", bufs=DEPTH["raw_i"], align_bytes=64)
            t["raw_i", which, k, n] = woven
            move = nc.vector.tensor_copy if engine == "vector" else nc.scalar.copy
            move(
                out=woven[:].rearrange("p (c i j) -> p c j i", i=4, j=PACK),
                in_=t["raw", which, k, n][:].rearrange("p j (c i) -> p c j i", i=4),
            )

        def quantize_operand(which, k, n):
            codes, scales = (w_codes, w_scales) if which == "w" else (h_codes, h_scales)
            cols = slice(n * N_TILE, (n + 1) * N_TILE)
            nc.vector.quantize_mx(
                out=codes[:, k, cols].bitcast(E4M3), scales=scales[:, k, cols], in_=t["raw_i", which, k, n][:]
            )

        def multiply(which, row, m, n):
            acc = psum.tile([P, N_TILE], F32, name="acc", bufs=DEPTH["acc"])
            t["acc", which, row, m, n] = acc
            passes = CHUNKS if which == "dh" else GROUPS
            m_cols = slice(m * P, (m + 1) * P)
            n_cols = slice(n * N_TILE, (n + 1) * N_TILE)
            for k in range(passes):
                if which == "dh":
                    dz_codes, dz_scales = fea_codes[:, row, k, m_cols], fea_scales[:, row, k, m_cols]
                    codes, scales = w_codes[:, k, n_cols], w_scales[:, k, n_cols]
                else:
                    dz_codes, dz_scales = tok_codes[:, k, row, m_cols], tok_scales[:, k, row, m_cols]
                    codes, scales = h_codes[:, k, n_cols], h_scales[:, k, n_cols]
                nc.tensor.matmul_mx(
                    out=acc[:],
                    lhsT=dz_codes.bitcast(E5M2),
                    lhsT_scale=dz_scales,
                    rhs=codes.bitcast(E4M3),
                    rhs_scale=scales,
                    start=(k == 0),
                    stop=(k == passes - 1),
                )

        def copy_out(which, row, m, n, engine):
            if ("stage", which, row, m) not in t:
                t["stage", which, row, m] = pool.tile([P, INCH], F32, name="stage", bufs=DEPTH["stage"])
            move = nc.vector.tensor_copy if engine == "vector" else nc.scalar.copy
            move(
                out=t["stage", which, row, m][:, n * N_TILE : (n + 1) * N_TILE],
                in_=t["acc", which, row, m, n][:],
            )

        def store(which, row, m, c0, c1):
            if which == "dh":
                hbm = dh_rows[rows(row), c0:c1].rearrange("(p j) n -> p j n", j=PACK)[:, m, :]
            else:
                first = row * K_PASS + m * P
                hbm = out_1[first : first + P, c0:c1]
            nc.sync.dma_start(out=hbm, in_=t["stage", which, row, m][:, c0:c1])

        tasks = []

        def task(name, engine, work, urgency, after, tiles, emit, *args):
            tasks.append((name, engine, work, urgency, after, tiles, lambda: emit(*args)))

        def columns(n):
            return START + n

        for q in range(GROUPS * CHUNKS // 2):
            g, pair = q // 2, q % 2
            work = BUS * 2 * PACK * 2 * K_PASS
            task(("grad", g, pair), "sync", work, 4 * q + GRAD_LAG, [], [("grad", g, pair)], load_grad, g, pair)

        finished = {}
        for s in range(STEPS):
            g, c, half = order[s]
            parts = ((0, 1), (1, 2)) if s in (0, LAST) else ((0, 2),)
            for a, e in parts if s == 0 else ((0, 2),):
                n = (e - a) * K_PASS
                tile = [("pre", s)]
                task(("load", s, a), "sync", BUS * 4 * n, s - PRE_LEAD, [], tile, load_pre, s, a, e)
                work, after = columns(n / 2), [("load", s, a)]
                task(("clamp", s, a), "vector", work, s - CLAMP_LEAD, after, tile, clamp, s, a, e)
            for a, e in parts:
                work, after = columns((e - a) * K_PASS), [("clamp", s, a if s == 0 else 0)]
                for k in range(4):
                    tiles = [("pre", s), ("gel%d" % k, s)]
                    task(("gelu", s, a, k), "scalar", work, s, after, tiles, gelu, s, a, e, k)

            def value(a, k):
                return ("gelu", s, a if len(parts) == 2 else 0, k)

            on_tensor = []
            for j in range(2):
                i = 2 * s + j
                if i < TENSOR_RANGE and (i + 1) * TENSOR_TILES // TENSOR_RANGE > i * TENSOR_TILES // TENSOR_RANGE:
                    on_tensor.append(j)
            if not on_tensor:
                vector_parts = parts
            else:
                vector_parts = [(j, j + 1) for j in range(2) if j not in on_tensor]
            done = []
            grad, dz_tiles = ("grad", g, c // 2), [("dz", g, c), ("grad", g, c // 2)]
            for j in on_tensor:
                after = [value(j, k) for k in range(4)]
                tiles = [("gel%d" % k, s) for k in range(4)] + [("sum", s, j)]
                task(("add", s, j), "tensor", 4 * MATMUL_F32, s, after, tiles, add_on_tensor, s, j)
                after, tiles = [("add", s, j), grad], dz_tiles + [("sum", s, j)]
                task(("dz", s, j), "vector", columns(K_PASS), s - URGENT, after, tiles, finish, s, j, j + 1, "sum")
                done.append(("dz", s, j))
            for a, e in vector_parts:
                work = columns((e - a) * K_PASS)
                after, tiles = [value(a, 0), value(a, 1)], [("gel0", s), ("gel1", s)]
                task(("near", s, a), "vector", work, s, after, tiles, subtract, s, a, e, "gel0", "gel1")
                after, tiles = [value(a, 2), value(a, 3)], [("gel2", s), ("gel3", s)]
                task(("far", s, a), "vector", work, s, after, tiles, subtract, s, a, e, "gel3", "gel2")
                after, tiles = [("near", s, a), ("far", s, a)], [("gel0", s), ("gel3", s)]
                task(("join", s, a), "vector", work, s, after, tiles, join, s, a, e)
                after, tiles = [("join", s, a), grad], dz_tiles + [("gel0", s)]
                task(("dz", s, a), "vector", work, s - URGENT, after, tiles, finish, s, a, e, "gel0")
                done.append(("dz", s, a))
            finished[s] = done

            tiles = [("words", s), ("dz", g, c)]
            task(("words", s), "tensor", 4 * TRANSPOSE, s, done, tiles, transpose_words, s)
            tiles = [("words", s), ("dz_fea", s)]
            task(("copy", s), "scalar", columns(K_PASS), s, [("words", s)], tiles, copy_words, s)
            tiles = [("dz_fea", s)]
            task(("features", s), "vector", columns(K_PASS / 2), s, [("copy", s)], tiles, quantize_features, s)
            if half == 1:
                width = K_PASS // 2 if s == LAST else K_PASS
                for f0 in range(0, K_PASS, width):
                    f1 = f0 + width
                    work, after = columns(WEAVE["vector"] * PACK * width), finished[step_of[g, c, 0]] + done
                    tiles = [("dz", g, c), ("dz_tok", g, c, f0)]
                    task(("weave", g, c, f0), "vector", work, s - URGENT, after, tiles, weave_tokens, g, c, f0, f1)
                    work, after, tiles = columns(width), [("weave", g, c, f0)], [("dz_tok", g, c, f0)]
                    task(("tokens", g, c, f0), "vector", work, s - URGENT, after, tiles, quantize_tokens, g, c, f0, f1)

        operands = [("w", k, n) for k in range(CHUNKS) for n in range(HALVES)]
        operands += [("h", k, n) for k in range(GROUPS) for n in range(HALVES)]
        for i in range(len(operands)):
            which, k, n = operands[i]
            urgency = 11 - i / 2 if which == "w" else 20 + 5 * (i - CHUNKS * HALVES)
            engine = "scalar" if i in (1, 3) else "vector"
            size, raw, woven = PACK * N_TILE, ("raw", which, k, n), ("raw_i", which, k, n)
            early = urgency - 1 if i > 0 else -5.0
            task(("load", which, k, n), "sync", BUS * 2 * size, early, [], [raw], load_operand, which, k, n)
            work, after = columns(WEAVE[engine] * size), [("load", which, k, n)]
            task(("weave", which, k, n), engine, work, urgency, after, [raw, woven], weave_operand, which, k, n, engine)
            work, after = columns(size / 4), [("weave", which, k, n)]
            task(("quantize", which, k, n), "vector", work, urgency + 1, after, [woven], quantize_operand, which, k, n)

        products = []
        for g in range(GROUPS):
            for m in range(PACK):
                steps = [step_of[g, c, m // 2] for c in range(CHUNKS)]
                for n in range(HALVES):
                    after = [("features", s) for s in steps] + [("quantize", "w", k, n) for k in range(CHUNKS)]
                    products.append((max(steps) - URGENT, "dh", g, m, n, after))
        for c in range(CHUNKS):
            for m in range(K_PASS // P):
                f0 = m // 2 * (K_PASS // 2) if c == last_chunk else 0
                for n in range(HALVES):
                    after = [("tokens", 0, c, 0), ("tokens", 1, c, f0)]
                    after += [("quantize", "h", k, n) for k in range(GROUPS)]
                    products.append((step_of[1, c, 1] - DW_LEAD, "dw", c, m, n, after))
        products = sorted(products, key=lambda product: product[:5])
        for i in range(len(products)):
            urgency, which, row, m, n, after = products[i]
            late = row == last_chunk if which == "dw" else row == 1 and m >= 2
            share = LATE_VECTOR_SHARE if late else VECTOR_SHARE
            engine = "vector" if i % share == share - 1 else "scalar"
            acc, stage = ("acc", which, row, m, n), ("stage", which, row, m)
            work = (CHUNKS if which == "dh" else GROUPS) * MATMUL_MX
            task(("multiply", which, row, m, n), "tensor", work, urgency, after, [acc], multiply, which, row, m, n)
            work, after = columns(N_TILE), [("multiply", which, row, m, n)]
            early = urgency - COPY_LEAD
            task(("out", which, row, m, n), engine, work, early, after, [acc, stage], copy_out, which, row, m, n, engine)
            if late:
                work, after, cols = BUS * 4 * N_TILE, [("out", which, row, m, n)], (n * N_TILE, (n + 1) * N_TILE)
            elif n == HALVES - 1:
                work, after, cols = BUS * 4 * INCH, [("out", which, row, m, i) for i in range(HALVES)], (0, INCH)
            if late or n == HALVES - 1:
                task(("store", which, row, m, n), "sync", work, urgency, after, [stage], store, which, row, m, *cols)

        for planned in plan(tasks):
            planned[6]()
